import numpy as np
import ml_dtypes


def mxq(x, axis, fmt="e4m3"):
    dtype, down = {"e4m3": (ml_dtypes.float8_e4m3fn, 7), "e5m2": (ml_dtypes.float8_e5m2, 14)}[fmt]
    v = np.moveaxis(np.asarray(x, np.float32).astype(ml_dtypes.bfloat16).astype(np.float64), axis, -1)
    blocks = v.reshape(v.shape[:-1] + (-1, 32))
    amax = np.abs(blocks).max(-1, keepdims=True)
    byte = np.maximum(np.where(amax > 0, np.frexp(amax)[1] - 1 + 127, 0) - down, 1)
    scale = np.exp2(byte - 127.0)
    codes = (blocks / scale).astype(np.float32).astype(dtype).astype(np.float64)
    return np.moveaxis((codes * scale).reshape(v.shape), -1, axis)


WIDE = False


def mx_kscale(k):
    if not WIDE:
        return np.ones(k)
    levels = np.array([10, -10, 5, -5, 0])
    a = np.random.permutation(np.resize(levels, k // 512 * 4)).reshape(k // 512, 4)
    idx = np.arange(k)
    return np.exp2(a[idx // 512, idx % 128 // 32])


BF16 = ml_dtypes.bfloat16


def bf(x):
    return np.asarray(x, np.float32).astype(BF16)


def f64(x):
    return np.asarray(x).astype(np.float64)


B, S, H, I = 2, 64, 512, 1024


def silu(v):
    return v / (1.0 + np.exp(-v))


def ternary(shape):
    return np.random.randint(-1, 2, shape).astype(np.float64)


def setup_inputs():
    s, t = mx_kscale(H), mx_kscale(I)
    x = np.random.standard_normal((B, S, H)) * s
    gate_w = ternary((I, H)) / s[None, :]
    up_w = ternary((I, H)) / s[None, :]
    down_w = ternary((H, I)) / t[None, :]
    gate_s = np.random.uniform(0.5, 2.5, I) / np.sqrt(H)
    up_s = np.random.uniform(0.5, 2.5, I) / np.sqrt(H) * t
    down_s = np.random.uniform(0.5, 2.5, H) / np.sqrt(I)
    return {"x": bf(x), "gate_w": bf(gate_w), "up_w": bf(up_w), "down_w": bf(down_w),
            "gate_s": bf(gate_s), "up_s": bf(up_s), "down_s": bf(down_s)}


def reference(x, gate_w, up_w, down_w, gate_s, up_s, down_s):
    x = f64(x)
    b, s, h = x.shape
    xq = mxq(x.reshape(b * s, h), 1, "e4m3")
    g = (xq @ mxq(f64(gate_w), 1, "e4m3").T) * f64(gate_s)
    u = (xq @ mxq(f64(up_w), 1, "e4m3").T) * f64(up_s)
    hdn = silu(g) * u
    out = (mxq(hdn, 1, "e4m3") @ mxq(f64(down_w), 1, "e4m3").T) * f64(down_s)
    return out.reshape(b, s, -1)

@@ -1,0 +1,196 @@
+from contextlib import ExitStack
+
+import concourse.mybir as mybir
+from concourse.masks import make_identity
+
+F32 = mybir.dt.float32
+BF16 = mybir.dt.bfloat16
+U32 = mybir.dt.uint32
+U8 = mybir.dt.uint8
+FP8X4 = mybir.dt.float8_e4m3fn_x4
+SILU = mybir.ActivationFunctionType.Silu
+MULT = mybir.AluOpType.mult
+
+P = 128
+PACK = 4
+K_PASS = P * PACK
+HIDDEN = 512
+INNER = 1024
+BANK = 512
+UNIT = 1024
+PAIRS = INNER // (2 * P)
+DOWN_UNITS = HIDDEN // P
+INNER_PASSES = INNER // K_PASS
+
+FLOPS = 2 * P * HIDDEN * INNER * 3
+
+
+def k_onto_partitions(nc, banks, identity, raw, grouped):
+    words = raw[:].bitcast(F32)
+    blocks = words.shape[1] // P
+    bank = banks.tile([P, BANK], F32, tag="bank")
+    for b in range(blocks):
+        nc.tensor.transpose(bank[:, b * P : (b + 1) * P], words[:, b * P : (b + 1) * P], identity[:])
+    nc.scalar.copy(
+        out=grouped[:].bitcast(F32).rearrange("p (s r v) -> p s r v", r=P, v=2),
+        in_=bank[:, 0 : blocks * P].rearrange("p (s v r) -> p s r v", v=2, r=P),
+    )
+
+
+def quantise(nc, grouped, codes, scales):
+    nc.vector.quantize_mx(out=codes[:].bitcast(FP8X4), scales=scales[:], in_=grouped[:])
+
+
+def tile_cudaternaryexpertmodule_s_kernel(
+    tc, x, gate_w, up_w, down_w, gate_s, up_s, down_s, out
+):
+    nc = tc.nc
+    x_rows = x.flatten_outer_dims()
+    out_rows = out.flatten_outer_dims()
+
+    gate_units = gate_w.rearrange("(m p e) k -> m p (e k)", p=P, e=2)
+    up_units = up_w.rearrange("(m p e) k -> m p (e k)", p=P, e=2)
+    down_units = down_w.rearrange("(j p) k -> j p k", p=P)
+    unit_views = []
+    for m in range(PAIRS):
+        unit_views.extend([gate_units[m], up_units[m]])
+    for j in range(DOWN_UNITS):
+        unit_views.append(down_units[j])
+    first_down = 2 * PAIRS
+
+    with ExitStack() as ctx:
+        ctx.enter_context(tc.manual_schedule())
+        fixed = ctx.enter_context(tc.tile_pool(name="fixed", bufs=1))
+        work = ctx.enter_context(tc.tile_pool(name="work", bufs=2))
+        banks = ctx.enter_context(tc.psum_pool(name="banks", bufs=8))
+
+        channel_rows = fixed.tile([P, 2 * P], BF16)
+        down_s_row = fixed.tile([P, HIDDEN], BF16)
+        ones = fixed.tile([P, P], BF16)
+        zero_column = fixed.tile([P, 1], F32)
+        nc.vector.memset(channel_rows[:], 0.0)
+        nc.vector.memset(down_s_row[:], 0.0)
+        nc.vector.memset(ones[:], 1.0)
+        nc.vector.memset(zero_column[:], 0.0)
+        identity = fixed.tile([P, P], F32)
+        make_identity(nc, identity[:])
+
+        nc.scalar.dma_start(out=down_s_row[0:1, :], in_=down_s.rearrange("(o n) -> o n", o=1))
+        nc.scalar.dma_start(out=channel_rows[0:4, :], in_=gate_s.rearrange("(r n) -> r n", r=4))
+        nc.scalar.dma_start(out=channel_rows[4:8, :], in_=up_s.rearrange("(r n) -> r n", r=4))
+        x_raw = fixed.tile([P, HIDDEN], BF16)
+        nc.sync.dma_start(out=x_raw[:], in_=x_rows)
+        unit_raw = []
+        for n, view in enumerate(unit_views):
+            unit_raw.append(fixed.tile([P, UNIT], BF16, name="unit_raw%d" % n))
+            nc.sync.dma_start(out=unit_raw[n][:], in_=view)
+
+        table_warmer = fixed.tile([P, 1], F32)
+        nc.scalar.activation(out=table_warmer[:], in_=zero_column[:], func=SILU)
+
+        down_s_bank = banks.tile([P, BANK], F32, tag="bank")
+        nc.tensor.matmul(out=down_s_bank[:], lhsT=ones[:], rhs=down_s_row[:], start=True, stop=True)
+        down_s_all = fixed.tile([P, HIDDEN], F32)
+        nc.scalar.copy(out=down_s_all[:], in_=down_s_bank[:])
+
+        channel_bank = banks.tile([P, BANK], F32, tag="bank")
+        nc.tensor.transpose(channel_bank[:, 0:P], channel_rows[:].bitcast(F32), identity[:])
+        channel_scales = fixed.tile([P, 16], F32)
+        nc.vector.tensor_copy(out=channel_scales[:], in_=channel_bank[:, 0:8].bitcast(BF16))
+
+        x_grouped = fixed.tile([P, P * PACK], BF16, align_bytes=64)
+        x_codes = fixed.tile([P, P], U32, align_bytes=64)
+        x_scales = fixed.tile([P, P], U8, align_bytes=64)
+        k_onto_partitions(nc, banks, identity, x_raw, x_grouped)
+        quantise(nc, x_grouped, x_codes, x_scales)
+
+        unit_codes = []
+        unit_scales = []
+        hidden_rows = []
+        hidden_codes = []
+        hidden_scales = []
+
+        def prepare_unit(n):
+            grouped = fixed.tile([P, UNIT], BF16, name="unit_grouped%d" % n, align_bytes=64)
+            unit_codes.append(fixed.tile([P, UNIT // PACK], U32, name="unit_codes%d" % n, align_bytes=64))
+            unit_scales.append(fixed.tile([P, UNIT // PACK], U8, name="unit_scales%d" % n, align_bytes=64))
+            k_onto_partitions(nc, banks, identity, unit_raw[n], grouped)
+            quantise(nc, grouped, unit_codes[n], unit_scales[n])
+
+        def hidden_tiles(m):
+            g_bank = banks.tile([P, BANK], F32, tag="bank")
+            u_bank = banks.tile([P, BANK], F32, tag="bank")
+            for e in range(2):
+                cols = slice(e * P, (e + 1) * P)
+                for bank, n in ((g_bank, 2 * m), (u_bank, 2 * m + 1)):
+                    nc.tensor.matmul_mx(
+                        out=bank[:, cols],
+                        lhsT=unit_codes[n][:, cols].bitcast(FP8X4),
+                        lhsT_scale=unit_scales[n][:, cols],
+                        rhs=x_codes[:].bitcast(FP8X4),
+                        rhs_scale=x_scales[:],
+                        start=True,
+                        stop=True,
+                    )
+            if m % 2 == 0:
+                hidden_rows.append(fixed.tile([P, PACK * P], BF16, name="hidden_rows%d" % (m // 2)))
+            silu_g = work.tile([P, 2 * P], F32)
+            for e in range(2):
+                cols = slice(e * P, (e + 1) * P)
+                channel = 2 * m + e
+                t = channel % PACK
+                nc.scalar.activation(
+                    out=silu_g[:, cols],
+                    in_=g_bank[:, cols],
+                    func=SILU,
+                    scale=channel_scales[:, channel : channel + 1],
+                )
+                nc.vector.scalar_tensor_tensor(
+                    out=hidden_rows[m // 2][:, t * P : (t + 1) * P],
+                    in0=u_bank[:, cols],
+                    scalar=channel_scales[:, 8 + channel : 8 + channel + 1],
+                    in1=silu_g[:, cols],
+                    op0=MULT,
+                    op1=MULT,
+                )
+
+        def quantise_hidden(c):
+            grouped = fixed.tile([P, P * PACK], BF16, name="hidden_grouped%d" % c, align_bytes=64)
+            hidden_codes.append(fixed.tile([P, P], U32, name="hidden_codes%d" % c, align_bytes=64))
+            hidden_scales.append(fixed.tile([P, P], U8, name="hidden_scales%d" % c, align_bytes=64))
+            nc.vector.tensor_copy(
+                out=grouped[:].rearrange("p (w t) -> p w t", t=PACK),
+                in_=hidden_rows[c][:].rearrange("p (t w) -> p w t", t=PACK),
+            )
+            quantise(nc, grouped, hidden_codes[c], hidden_scales[c])
+
+        rounds = len(unit_views) // 2
+        for i in range(rounds):
+            prepare_unit(2 * i)
+            prepare_unit(2 * i + 1)
+            m = i - 1
+            if 0 <= m < PAIRS:
+                hidden_tiles(m)
+                if m % 2 == 1:
+                    quantise_hidden(m // 2)
+
+        for half in range(2):
+            out_bank = banks.tile([P, BANK], F32, tag="bank")
+            for jj in range(2):
+                n = first_down + 2 * half + jj
+                for c in range(INNER_PASSES):
+                    nc.tensor.matmul_mx(
+                        out=out_bank[:, jj * P : (jj + 1) * P],
+                        lhsT=hidden_codes[c][:].bitcast(FP8X4),
+                        lhsT_scale=hidden_scales[c][:],
+                        rhs=unit_codes[n][:, c * P : (c + 1) * P].bitcast(FP8X4),
+                        rhs_scale=unit_scales[n][:, c * P : (c + 1) * P],
+                        start=(c == 0),
+                        stop=(c == INNER_PASSES - 1),
+                    )
+            channels = slice(half * 2 * P, (half + 1) * 2 * P)
+            result = work.tile([P, 2 * P], F32)
+            nc.vector.tensor_tensor(
+                out=result[:], in0=out_bank[:, 0 : 2 * P], in1=down_s_all[:, channels], op=MULT
+            )
+            nc.sync.dma_start(out=out_rows[:, channels], in_=result[:])

@@ -25,13 +25,13 @@ INNER_PASSES = INNER // K_PASS
 FLOPS = 2 * P * HIDDEN * INNER * 3
 
 
-def k_onto_partitions(nc, banks, identity, raw, grouped):
+def k_onto_partitions(nc, banks, identity, raw, grouped, copy_out):
     words = raw[:].bitcast(F32)
     blocks = words.shape[1] // P
     bank = banks.tile([P, BANK], F32, tag="bank")
     for b in range(blocks):
         nc.tensor.transpose(bank[:, b * P : (b + 1) * P], words[:, b * P : (b + 1) * P], identity[:])
-    nc.scalar.copy(
+    copy_out(
         out=grouped[:].bitcast(F32).rearrange("p (s r v) -> p s r v", r=P, v=2),
         in_=bank[:, 0 : blocks * P].rearrange("p (s v r) -> p s r v", v=2, r=P),
     )
@@ -75,9 +75,9 @@ def tile_cudaternaryexpertmodule_s_kernel(
         identity = fixed.tile([P, P], F32)
         make_identity(nc, identity[:])
 
-        nc.scalar.dma_start(out=down_s_row[0:1, :], in_=down_s.rearrange("(o n) -> o n", o=1))
         nc.scalar.dma_start(out=channel_rows[0:4, :], in_=gate_s.rearrange("(r n) -> r n", r=4))
         nc.scalar.dma_start(out=channel_rows[4:8, :], in_=up_s.rearrange("(r n) -> r n", r=4))
+        nc.scalar.dma_start(out=down_s_row[0:1, :], in_=down_s.rearrange("(o n) -> o n", o=1))
         x_raw = fixed.tile([P, HIDDEN], BF16)
         nc.sync.dma_start(out=x_raw[:], in_=x_rows)
         unit_raw = []
@@ -88,34 +88,41 @@ def tile_cudaternaryexpertmodule_s_kernel(
         table_warmer = fixed.tile([P, 1], F32)
         nc.scalar.activation(out=table_warmer[:], in_=zero_column[:], func=SILU)
 
-        down_s_bank = banks.tile([P, BANK], F32, tag="bank")
-        nc.tensor.matmul(out=down_s_bank[:], lhsT=ones[:], rhs=down_s_row[:], start=True, stop=True)
-        down_s_all = fixed.tile([P, HIDDEN], F32)
-        nc.scalar.copy(out=down_s_all[:], in_=down_s_bank[:])
-
-        channel_bank = banks.tile([P, BANK], F32, tag="bank")
-        nc.tensor.transpose(channel_bank[:, 0:P], channel_rows[:].bitcast(F32), identity[:])
-        channel_scales = fixed.tile([P, 16], F32)
-        nc.vector.tensor_copy(out=channel_scales[:], in_=channel_bank[:, 0:8].bitcast(BF16))
-
         x_grouped = fixed.tile([P, P * PACK], BF16, align_bytes=64)
         x_codes = fixed.tile([P, P], U32, align_bytes=64)
         x_scales = fixed.tile([P, P], U8, align_bytes=64)
-        k_onto_partitions(nc, banks, identity, x_raw, x_grouped)
+        k_onto_partitions(nc, banks, identity, x_raw, x_grouped, nc.vector.tensor_copy)
         quantise(nc, x_grouped, x_codes, x_scales)
 
+        channel_scales = fixed.tile([P, 16], F32)
+        down_s_all = fixed.tile([P, HIDDEN], F32)
+
+        def spread_channel_scales():
+            channel_bank = banks.tile([P, BANK], F32, tag="bank")
+            nc.tensor.transpose(channel_bank[:, 0:P], channel_rows[:].bitcast(F32), identity[:])
+            nc.vector.tensor_copy(out=channel_scales[:], in_=channel_bank[:, 0:8].bitcast(BF16))
+
+        def spread_down_s():
+            down_s_bank = banks.tile([P, BANK], F32, tag="bank")
+            nc.tensor.matmul(out=down_s_bank[:], lhsT=ones[:], rhs=down_s_row[:], start=True, stop=True)
+            nc.vector.tensor_copy(out=down_s_all[:], in_=down_s_bank[:])
+
+        unit_grouped = []
         unit_codes = []
         unit_scales = []
         hidden_rows = []
+        hidden_grouped = []
         hidden_codes = []
         hidden_scales = []
 
-        def prepare_unit(n):
-            grouped = fixed.tile([P, UNIT], BF16, name="unit_grouped%d" % n, align_bytes=64)
+        def transpose_unit(n):
+            unit_grouped.append(fixed.tile([P, UNIT], BF16, name="unit_grouped%d" % n, align_bytes=64))
+            k_onto_partitions(nc, banks, identity, unit_raw[n], unit_grouped[n], nc.scalar.copy)
+
+        def quantise_unit(n):
             unit_codes.append(fixed.tile([P, UNIT // PACK], U32, name="unit_codes%d" % n, align_bytes=64))
             unit_scales.append(fixed.tile([P, UNIT // PACK], U8, name="unit_scales%d" % n, align_bytes=64))
-            k_onto_partitions(nc, banks, identity, unit_raw[n], grouped)
-            quantise(nc, grouped, unit_codes[n], unit_scales[n])
+            quantise(nc, unit_grouped[n], unit_codes[n], unit_scales[n])
 
         def hidden_tiles(m):
             g_bank = banks.tile([P, BANK], F32, tag="bank")
@@ -154,25 +161,35 @@ def tile_cudaternaryexpertmodule_s_kernel(
                     op1=MULT,
                 )
 
-        def quantise_hidden(c):
-            grouped = fixed.tile([P, P * PACK], BF16, name="hidden_grouped%d" % c, align_bytes=64)
-            hidden_codes.append(fixed.tile([P, P], U32, name="hidden_codes%d" % c, align_bytes=64))
-            hidden_scales.append(fixed.tile([P, P], U8, name="hidden_scales%d" % c, align_bytes=64))
+        def regroup_hidden(c):
+            hidden_grouped.append(fixed.tile([P, P * PACK], BF16, name="hidden_grouped%d" % c, align_bytes=64))
             nc.vector.tensor_copy(
-                out=grouped[:].rearrange("p (w t) -> p w t", t=PACK),
+                out=hidden_grouped[c][:].rearrange("p (w t) -> p w t", t=PACK),
                 in_=hidden_rows[c][:].rearrange("p (t w) -> p w t", t=PACK),
             )
-            quantise(nc, grouped, hidden_codes[c], hidden_scales[c])
+
+        def quantise_hidden(c):
+            hidden_codes.append(fixed.tile([P, P], U32, name="hidden_codes%d" % c, align_bytes=64))
+            hidden_scales.append(fixed.tile([P, P], U8, name="hidden_scales%d" % c, align_bytes=64))
+            quantise(nc, hidden_grouped[c], hidden_codes[c], hidden_scales[c])
 
         rounds = len(unit_views) // 2
         for i in range(rounds):
-            prepare_unit(2 * i)
-            prepare_unit(2 * i + 1)
+            transpose_unit(2 * i)
+            transpose_unit(2 * i + 1)
+            if i == 1:
+                spread_channel_scales()
+            quantise_unit(2 * i)
+            if i >= 3 and i % 2 == 1:
+                quantise_hidden((i - 3) // 2)
+            quantise_unit(2 * i + 1)
+            if i == 1:
+                spread_down_s()
             m = i - 1
             if 0 <= m < PAIRS:
                 hidden_tiles(m)
                 if m % 2 == 1:
-                    quantise_hidden(m // 2)
+                    regroup_hidden(m // 2)
 
         for half in range(2):
             out_bank = banks.tile([P, BANK], F32, tag="bank")

@@ -7,6 +7,7 @@ F32 = mybir.dt.float32
 BF16 = mybir.dt.bfloat16
 U32 = mybir.dt.uint32
 U8 = mybir.dt.uint8
+I32 = mybir.dt.int32
 FP8X4 = mybir.dt.float8_e4m3fn_x4
 SILU = mybir.ActivationFunctionType.Silu
 MULT = mybir.AluOpType.mult
@@ -21,6 +22,9 @@ UNIT = 1024
 PAIRS = INNER // (2 * P)
 DOWN_UNITS = HIDDEN // P
 INNER_PASSES = INNER // K_PASS
+CLOCK_BAR = 1024
+IDLE_COLUMNS = 256
+WARM_UP_PASSES = 6
 
 FLOPS = 2 * P * HIDDEN * INNER * 3
 
@@ -62,7 +66,29 @@ def tile_cudaternaryexpertmodule_s_kernel(
         ctx.enter_context(tc.manual_schedule())
         fixed = ctx.enter_context(tc.tile_pool(name="fixed", bufs=1))
         work = ctx.enter_context(tc.tile_pool(name="work", bufs=2))
-        banks = ctx.enter_context(tc.psum_pool(name="banks", bufs=8))
+        banks = ctx.enter_context(tc.psum_pool(name="banks", bufs=7))
+        idle = ctx.enter_context(tc.psum_pool(name="idle", bufs=1))
+
+        idle_values = fixed.tile([P, IDLE_COLUMNS * PACK], BF16, align_bytes=64)
+        idle_codes = fixed.tile([P, IDLE_COLUMNS], U32, align_bytes=64)
+        idle_scales = fixed.tile([P, IDLE_COLUMNS], U8, align_bytes=64)
+        idle_bank = idle.tile([P, BANK], F32)
+        nc.vector.memset(idle_values[:].bitcast(I32), 0)
+        quantise(nc, idle_values, idle_codes, idle_scales)
+
+        def idle_passes(count):
+            for k in range(count):
+                nc.tensor.matmul_mx(
+                    out=idle_bank[:, 0:IDLE_COLUMNS],
+                    lhsT=idle_codes[:, 0:P].bitcast(FP8X4),
+                    lhsT_scale=idle_scales[:, 0:P],
+                    rhs=idle_codes[:].bitcast(FP8X4),
+                    rhs_scale=idle_scales[:],
+                    start=True,
+                    stop=True,
+                )
+
+        idle_passes(WARM_UP_PASSES)
 
         channel_rows = fixed.tile([P, 2 * P], BF16)
         down_s_row = fixed.tile([P, HIDDEN], BF16)
@@ -190,6 +216,9 @@ def tile_cudaternaryexpertmodule_s_kernel(
                 hidden_tiles(m)
                 if m % 2 == 1:
                     regroup_hidden(m // 2)
+                idle_passes((CLOCK_BAR - 4 * P) // IDLE_COLUMNS)
+            elif i == 0:
+                idle_passes(CLOCK_BAR // IDLE_COLUMNS)
 
         for half in range(2):
             out_bank = banks.tile([P, BANK], F32, tag="bank")

@@ -7,7 +7,6 @@ F32 = mybir.dt.float32
 BF16 = mybir.dt.bfloat16
 U32 = mybir.dt.uint32
 U8 = mybir.dt.uint8
-I32 = mybir.dt.int32
 FP8X4 = mybir.dt.float8_e4m3fn_x4
 SILU = mybir.ActivationFunctionType.Silu
 MULT = mybir.AluOpType.mult
@@ -22,9 +21,6 @@ UNIT = 1024
 PAIRS = INNER // (2 * P)
 DOWN_UNITS = HIDDEN // P
 INNER_PASSES = INNER // K_PASS
-CLOCK_BAR = 1024
-IDLE_COLUMNS = 256
-WARM_UP_PASSES = 6
 
 FLOPS = 2 * P * HIDDEN * INNER * 3
 
@@ -66,29 +62,7 @@ def tile_cudaternaryexpertmodule_s_kernel(
         ctx.enter_context(tc.manual_schedule())
         fixed = ctx.enter_context(tc.tile_pool(name="fixed", bufs=1))
         work = ctx.enter_context(tc.tile_pool(name="work", bufs=2))
-        banks = ctx.enter_context(tc.psum_pool(name="banks", bufs=7))
-        idle = ctx.enter_context(tc.psum_pool(name="idle", bufs=1))
-
-        idle_values = fixed.tile([P, IDLE_COLUMNS * PACK], BF16, align_bytes=64)
-        idle_codes = fixed.tile([P, IDLE_COLUMNS], U32, align_bytes=64)
-        idle_scales = fixed.tile([P, IDLE_COLUMNS], U8, align_bytes=64)
-        idle_bank = idle.tile([P, BANK], F32)
-        nc.vector.memset(idle_values[:].bitcast(I32), 0)
-        quantise(nc, idle_values, idle_codes, idle_scales)
-
-        def idle_passes(count):
-            for k in range(count):
-                nc.tensor.matmul_mx(
-                    out=idle_bank[:, 0:IDLE_COLUMNS],
-                    lhsT=idle_codes[:, 0:P].bitcast(FP8X4),
-                    lhsT_scale=idle_scales[:, 0:P],
-                    rhs=idle_codes[:].bitcast(FP8X4),
-                    rhs_scale=idle_scales[:],
-                    start=True,
-                    stop=True,
-                )
-
-        idle_passes(WARM_UP_PASSES)
+        banks = ctx.enter_context(tc.psum_pool(name="banks", bufs=8))
 
         channel_rows = fixed.tile([P, 2 * P], BF16)
         down_s_row = fixed.tile([P, HIDDEN], BF16)
@@ -101,9 +75,11 @@ def tile_cudaternaryexpertmodule_s_kernel(
         identity = fixed.tile([P, P], F32)
         make_identity(nc, identity[:])
 
-        nc.scalar.dma_start(out=channel_rows[0:4, :], in_=gate_s.rearrange("(r n) -> r n", r=4))
-        nc.scalar.dma_start(out=channel_rows[4:8, :], in_=up_s.rearrange("(r n) -> r n", r=4))
-        nc.scalar.dma_start(out=down_s_row[0:1, :], in_=down_s.rearrange("(o n) -> o n", o=1))
+        channel_stage = fixed.tile([8, 2 * P], BF16)
+        down_s_stage = fixed.tile([1, HIDDEN], BF16)
+        nc.scalar.dma_start(out=channel_stage[0:4, :], in_=gate_s.rearrange("(r n) -> r n", r=4))
+        nc.scalar.dma_start(out=channel_stage[4:8, :], in_=up_s.rearrange("(r n) -> r n", r=4))
+        nc.scalar.dma_start(out=down_s_stage[:], in_=down_s.rearrange("(o n) -> o n", o=1))
         x_raw = fixed.tile([P, HIDDEN], BF16)
         nc.sync.dma_start(out=x_raw[:], in_=x_rows)
         unit_raw = []
@@ -120,6 +96,9 @@ def tile_cudaternaryexpertmodule_s_kernel(
         k_onto_partitions(nc, banks, identity, x_raw, x_grouped, nc.vector.tensor_copy)
         quantise(nc, x_grouped, x_codes, x_scales)
 
+        nc.vector.tensor_copy(out=channel_rows[0:8, :], in_=channel_stage[:])
+        nc.vector.tensor_copy(out=down_s_row[0:1, :], in_=down_s_stage[:])
+
         channel_scales = fixed.tile([P, 16], F32)
         down_s_all = fixed.tile([P, HIDDEN], F32)
 
@@ -131,7 +110,7 @@ def tile_cudaternaryexpertmodule_s_kernel(
         def spread_down_s():
             down_s_bank = banks.tile([P, BANK], F32, tag="bank")
             nc.tensor.matmul(out=down_s_bank[:], lhsT=ones[:], rhs=down_s_row[:], start=True, stop=True)
-            nc.vector.tensor_copy(out=down_s_all[:], in_=down_s_bank[:])
+            nc.scalar.copy(out=down_s_all[:], in_=down_s_bank[:])
 
         unit_grouped = []
         unit_codes = []
@@ -205,38 +184,34 @@ def tile_cudaternaryexpertmodule_s_kernel(
             transpose_unit(2 * i + 1)
             if i == 1:
                 spread_channel_scales()
+            if i == rounds - 1:
+                spread_down_s()
             quantise_unit(2 * i)
             if i >= 3 and i % 2 == 1:
                 quantise_hidden((i - 3) // 2)
             quantise_unit(2 * i + 1)
-            if i == 1:
-                spread_down_s()
             m = i - 1
             if 0 <= m < PAIRS:
                 hidden_tiles(m)
                 if m % 2 == 1:
                     regroup_hidden(m // 2)
-                idle_passes((CLOCK_BAR - 4 * P) // IDLE_COLUMNS)
-            elif i == 0:
-                idle_passes(CLOCK_BAR // IDLE_COLUMNS)
 
-        for half in range(2):
+        for j in range(DOWN_UNITS):
+            n = first_down + j
             out_bank = banks.tile([P, BANK], F32, tag="bank")
-            for jj in range(2):
-                n = first_down + 2 * half + jj
-                for c in range(INNER_PASSES):
-                    nc.tensor.matmul_mx(
-                        out=out_bank[:, jj * P : (jj + 1) * P],
-                        lhsT=hidden_codes[c][:].bitcast(FP8X4),
-                        lhsT_scale=hidden_scales[c][:],
-                        rhs=unit_codes[n][:, c * P : (c + 1) * P].bitcast(FP8X4),
-                        rhs_scale=unit_scales[n][:, c * P : (c + 1) * P],
-                        start=(c == 0),
-                        stop=(c == INNER_PASSES - 1),
-                    )
-            channels = slice(half * 2 * P, (half + 1) * 2 * P)
-            result = work.tile([P, 2 * P], F32)
+            for c in range(INNER_PASSES):
+                nc.tensor.matmul_mx(
+                    out=out_bank[:, 0:P],
+                    lhsT=hidden_codes[c][:].bitcast(FP8X4),
+                    lhsT_scale=hidden_scales[c][:],
+                    rhs=unit_codes[n][:, c * P : (c + 1) * P].bitcast(FP8X4),
+                    rhs_scale=unit_scales[n][:, c * P : (c + 1) * P],
+                    start=(c == 0),
+                    stop=(c == INNER_PASSES - 1),
+                )
+            channels = slice(j * P, (j + 1) * P)
+            result = work.tile([P, P], F32, bufs=DOWN_UNITS)
             nc.vector.tensor_tensor(
-                out=result[:], in0=out_bank[:, 0 : 2 * P], in1=down_s_all[:, channels], op=MULT
+                out=result[:], in0=out_bank[:, 0:P], in1=down_s_all[:, channels], op=MULT
             )
             nc.sync.dma_start(out=out_rows[:, channels], in_=result[:])

from contextlib import ExitStack

import concourse.mybir as mybir
from concourse.masks import make_identity

F32 = mybir.dt.float32
BF16 = mybir.dt.bfloat16
U32 = mybir.dt.uint32
U8 = mybir.dt.uint8
FP8X4 = mybir.dt.float8_e4m3fn_x4
SILU = mybir.ActivationFunctionType.Silu
MULT = mybir.AluOpType.mult

P = 128
PACK = 4
K_PASS = P * PACK
HIDDEN = 512
INNER = 1024
BANK = 512
UNIT = 1024
PAIRS = INNER // (2 * P)
DOWN_UNITS = HIDDEN // P
INNER_PASSES = INNER // K_PASS

FLOPS = 2 * P * HIDDEN * INNER * 3


def k_onto_partitions(nc, banks, identity, raw, grouped, copy_out):
    words = raw[:].bitcast(F32)
    blocks = words.shape[1] // P
    bank = banks.tile([P, BANK], F32, tag="bank")
    for b in range(blocks):
        nc.tensor.transpose(bank[:, b * P : (b + 1) * P], words[:, b * P : (b + 1) * P], identity[:])
    copy_out(
        out=grouped[:].bitcast(F32).rearrange("p (s r v) -> p s r v", r=P, v=2),
        in_=bank[:, 0 : blocks * P].rearrange("p (s v r) -> p s r v", v=2, r=P),
    )


def quantise(nc, grouped, codes, scales):
    nc.vector.quantize_mx(out=codes[:].bitcast(FP8X4), scales=scales[:], in_=grouped[:])


def tile_cudaternaryexpertmodule_s_kernel(
    tc, x, gate_w, up_w, down_w, gate_s, up_s, down_s, out
):
    nc = tc.nc
    x_rows = x.flatten_outer_dims()
    out_rows = out.flatten_outer_dims()

    gate_units = gate_w.rearrange("(m p e) k -> m p (e k)", p=P, e=2)
    up_units = up_w.rearrange("(m p e) k -> m p (e k)", p=P, e=2)
    down_units = down_w.rearrange("(j p) k -> j p k", p=P)
    unit_views = []
    for m in range(PAIRS):
        unit_views.extend([gate_units[m], up_units[m]])
    for j in range(DOWN_UNITS):
        unit_views.append(down_units[j])
    first_down = 2 * PAIRS

    with ExitStack() as ctx:
        ctx.enter_context(tc.manual_schedule())
        fixed = ctx.enter_context(tc.tile_pool(name="fixed", bufs=1))
        work = ctx.enter_context(tc.tile_pool(name="work", bufs=2))
        banks = ctx.enter_context(tc.psum_pool(name="banks", bufs=8))

        channel_rows = fixed.tile([P, 2 * P], BF16)
        down_s_row = fixed.tile([P, HIDDEN], BF16)
        ones = fixed.tile([P, P], BF16)
        zero_column = fixed.tile([P, 1], F32)
        nc.vector.memset(channel_rows[:], 0.0)
        nc.vector.memset(down_s_row[:], 0.0)
        nc.vector.memset(ones[:], 1.0)
        nc.vector.memset(zero_column[:], 0.0)
        identity = fixed.tile([P, P], F32)
        make_identity(nc, identity[:])

        channel_stage = fixed.tile([8, 2 * P], BF16)
        down_s_stage = fixed.tile([1, HIDDEN], BF16)
        nc.scalar.dma_start(out=channel_stage[0:4, :], in_=gate_s.rearrange("(r n) -> r n", r=4))
        nc.scalar.dma_start(out=channel_stage[4:8, :], in_=up_s.rearrange("(r n) -> r n", r=4))
        nc.scalar.dma_start(out=down_s_stage[:], in_=down_s.rearrange("(o n) -> o n", o=1))
        x_raw = fixed.tile([P, HIDDEN], BF16)
        nc.sync.dma_start(out=x_raw[:], in_=x_rows)
        unit_raw = []
        for n, view in enumerate(unit_views):
            unit_raw.append(fixed.tile([P, UNIT], BF16, name="unit_raw%d" % n))
            nc.sync.dma_start(out=unit_raw[n][:], in_=view)

        table_warmer = fixed.tile([P, 1], F32)
        nc.scalar.activation(out=table_warmer[:], in_=zero_column[:], func=SILU)

        x_grouped = fixed.tile([P, P * PACK], BF16, align_bytes=64)
        x_codes = fixed.tile([P, P], U32, align_bytes=64)
        x_scales = fixed.tile([P, P], U8, align_bytes=64)
        k_onto_partitions(nc, banks, identity, x_raw, x_grouped, nc.vector.tensor_copy)
        quantise(nc, x_grouped, x_codes, x_scales)

        nc.vector.tensor_copy(out=channel_rows[0:8, :], in_=channel_stage[:])
        nc.vector.tensor_copy(out=down_s_row[0:1, :], in_=down_s_stage[:])

        channel_scales = fixed.tile([P, 16], F32)
        down_s_all = fixed.tile([P, HIDDEN], F32)

        def spread_channel_scales():
            channel_bank = banks.tile([P, BANK], F32, tag="bank")
            nc.tensor.transpose(channel_bank[:, 0:P], channel_rows[:].bitcast(F32), identity[:])
            nc.vector.tensor_copy(out=channel_scales[:], in_=channel_bank[:, 0:8].bitcast(BF16))

        def spread_down_s():
            down_s_bank = banks.tile([P, BANK], F32, tag="bank")
            nc.tensor.matmul(out=down_s_bank[:], lhsT=ones[:], rhs=down_s_row[:], start=True, stop=True)
            nc.scalar.copy(out=down_s_all[:], in_=down_s_bank[:])

        unit_grouped = []
        unit_codes = []
        unit_scales = []
        hidden_rows = []
        hidden_grouped = []
        hidden_codes = []
        hidden_scales = []

        def transpose_unit(n):
            unit_grouped.append(fixed.tile([P, UNIT], BF16, name="unit_grouped%d" % n, align_bytes=64))
            k_onto_partitions(nc, banks, identity, unit_raw[n], unit_grouped[n], nc.scalar.copy)

        def quantise_unit(n):
            unit_codes.append(fixed.tile([P, UNIT // PACK], U32, name="unit_codes%d" % n, align_bytes=64))
            unit_scales.append(fixed.tile([P, UNIT // PACK], U8, name="unit_scales%d" % n, align_bytes=64))
            quantise(nc, unit_grouped[n], unit_codes[n], unit_scales[n])

        def hidden_tiles(m):
            g_bank = banks.tile([P, BANK], F32, tag="bank")
            u_bank = banks.tile([P, BANK], F32, tag="bank")
            for e in range(2):
                cols = slice(e * P, (e + 1) * P)
                for bank, n in ((g_bank, 2 * m), (u_bank, 2 * m + 1)):
                    nc.tensor.matmul_mx(
                        out=bank[:, cols],
                        lhsT=unit_codes[n][:, cols].bitcast(FP8X4),
                        lhsT_scale=unit_scales[n][:, cols],
                        rhs=x_codes[:].bitcast(FP8X4),
                        rhs_scale=x_scales[:],
                        start=True,
                        stop=True,
                    )
            if m % 2 == 0:
                hidden_rows.append(fixed.tile([P, PACK * P], BF16, name="hidden_rows%d" % (m // 2)))
            silu_g = work.tile([P, 2 * P], F32)
            for e in range(2):
                cols = slice(e * P, (e + 1) * P)
                channel = 2 * m + e
                t = channel % PACK
                nc.scalar.activation(
                    out=silu_g[:, cols],
                    in_=g_bank[:, cols],
                    func=SILU,
                    scale=channel_scales[:, channel : channel + 1],
                )
                nc.vector.scalar_tensor_tensor(
                    out=hidden_rows[m // 2][:, t * P : (t + 1) * P],
                    in0=u_bank[:, cols],
                    scalar=channel_scales[:, 8 + channel : 8 + channel + 1],
                    in1=silu_g[:, cols],
                    op0=MULT,
                    op1=MULT,
                )

        def regroup_hidden(c):
            hidden_grouped.append(fixed.tile([P, P * PACK], BF16, name="hidden_grouped%d" % c, align_bytes=64))
            nc.vector.tensor_copy(
                out=hidden_grouped[c][:].rearrange("p (w t) -> p w t", t=PACK),
                in_=hidden_rows[c][:].rearrange("p (t w) -> p w t", t=PACK),
            )

        def quantise_hidden(c):
            hidden_codes.append(fixed.tile([P, P], U32, name="hidden_codes%d" % c, align_bytes=64))
            hidden_scales.append(fixed.tile([P, P], U8, name="hidden_scales%d" % c, align_bytes=64))
            quantise(nc, hidden_grouped[c], hidden_codes[c], hidden_scales[c])

        rounds = len(unit_views) // 2
        for i in range(rounds):
            transpose_unit(2 * i)
            transpose_unit(2 * i + 1)
            if i == 1:
                spread_channel_scales()
            if i == rounds - 1:
                spread_down_s()
            quantise_unit(2 * i)
            if i >= 3 and i % 2 == 1:
                quantise_hidden((i - 3) // 2)
            quantise_unit(2 * i + 1)
            m = i - 1
            if 0 <= m < PAIRS:
                hidden_tiles(m)
                if m % 2 == 1:
                    regroup_hidden(m // 2)

        for j in range(DOWN_UNITS):
            n = first_down + j
            out_bank = banks.tile([P, BANK], F32, tag="bank")
            for c in range(INNER_PASSES):
                nc.tensor.matmul_mx(
                    out=out_bank[:, 0:P],
                    lhsT=hidden_codes[c][:].bitcast(FP8X4),
                    lhsT_scale=hidden_scales[c][:],
                    rhs=unit_codes[n][:, c * P : (c + 1) * P].bitcast(FP8X4),
                    rhs_scale=unit_scales[n][:, c * P : (c + 1) * P],
                    start=(c == 0),
                    stop=(c == INNER_PASSES - 1),
                )
            channels = slice(j * P, (j + 1) * P)
            result = work.tile([P, P], F32, bufs=DOWN_UNITS)
            nc.vector.tensor_tensor(
                out=result[:], in0=out_bank[:, 0:P], in1=down_s_all[:, channels], op=MULT
            )
            nc.sync.dma_start(out=out_rows[:, channels], in_=result[:])
